import numpy as np
import ml_dtypes


def mxq(x, axis, fmt="e4m3"):
    dtype, down = {"e4m3": (ml_dtypes.float8_e4m3fn, 7), "e5m2": (ml_dtypes.float8_e5m2, 14)}[fmt]
    v = np.moveaxis(np.asarray(x, np.float32).astype(ml_dtypes.bfloat16).astype(np.float64), axis, -1)
    blocks = v.reshape(v.shape[:-1] + (-1, 32))
    amax = np.abs(blocks).max(-1, keepdims=True)
    byte = np.maximum(np.where(amax > 0, np.frexp(amax)[1] - 1 + 127, 0) - down, 1)
    scale = np.exp2(byte - 127.0)
    codes = (blocks / scale).astype(np.float32).astype(dtype).astype(np.float64)
    return np.moveaxis((codes * scale).reshape(v.shape), -1, axis)


WIDE = False


def mx_kscale(k):
    if not WIDE:
        return np.ones(k)
    levels = np.array([10, -10, 5, -5, 0])
    a = np.random.permutation(np.resize(levels, k // 512 * 4)).reshape(k // 512, 4)
    idx = np.arange(k)
    return np.exp2(a[idx // 512, idx % 128 // 32])


BF16 = ml_dtypes.bfloat16


def bf(x):
    return np.asarray(x, np.float32).astype(BF16)


def f64(x):
    return np.asarray(x).astype(np.float64)


E2M1 = np.array([0.0, 0.5, 1.0, 1.5, 2.0, 3.0, 4.0, 6.0, -0.0, -0.5, -1.0, -1.5, -2.0, -3.0, -4.0, -6.0])


def pack_weight(w, fmt):
    k, n = w.shape
    w = f64(bf(w)).reshape(k // 32, 32, n)
    amax = np.abs(w).max(1)
    if fmt == "e4m3":
        byte = np.frexp(amax)[1] - 1 + 127 - 7
    else:
        mant, ex = np.frexp(amax / 6.0)
        byte = np.where(mant > 0.5, ex, ex - 1) + 127
    byte = np.clip(np.where(amax > 0, byte, 1), 1, 254)
    scaled = (w * np.exp2(127.0 - byte)[:, None, :]).reshape(k, n).astype(np.float32)
    by_word = np.ascontiguousarray(scaled.reshape(k // 512, 128, 4, n).transpose(0, 1, 3, 2))
    if fmt == "e4m3":
        words = by_word.astype(ml_dtypes.float8_e4m3fn).view(np.uint8)
    else:
        c = by_word.astype(ml_dtypes.float4_e2m1fn).view(np.uint8) & 0xF
        words = c[..., 0::2] | (c[..., 1::2] << 4)
    return np.ascontiguousarray(words), np.ascontiguousarray(byte.astype(np.uint8).reshape(k // 512, 16, n))


def unpack_weight(words, scales, fmt):
    g, p, n, _ = words.shape
    if fmt == "e4m3":
        vals = np.ascontiguousarray(words).view(ml_dtypes.float8_e4m3fn).astype(np.float64)
    else:
        nib = np.empty((g, p, n, 4), np.uint8)
        nib[..., 0::2] = words & 0xF
        nib[..., 1::2] = words >> 4
        vals = E2M1[nib]
    vals = vals * np.repeat(np.exp2(scales.astype(np.float64) - 127.0), 8, axis=1)[..., None]
    return vals.transpose(0, 1, 3, 2).reshape(g * 512, n)

def pack4(w):
    words, scales = pack_weight(w, "e2m1")
    return words.reshape(words.shape[0], 128, -1), scales


def unpack4(words, scales):
    return unpack_weight(words.reshape(words.shape[0], 128, -1, 2), scales, "e2m1")


B, T, S, H, C, CO, W = 2, 128, 16, 8, 1024, 1024, 5
HD = C // H


def setup_inputs():
    t = mx_kscale(C)
    i = np.arange(T)
    band = np.abs(i[:, None] - i[None, :]) <= W
    e = np.exp(np.random.standard_normal((B, H, S, T, T))) * band
    attn = bf(e / e.sum(-1, keepdims=True))
    v = bf(np.random.standard_normal((B, T, S, H, HD)) * t.reshape(H, HD))
    words, scales = pack4(np.random.standard_normal((C, CO)) / np.sqrt(C) / t[:, None])
    return {"attn": attn,
            "v": v,
            "W_out_words": words,
            "W_out_scales": scales}


def reference(attn, v, W_out_words, W_out_scales):
    ctx = f64(attn) @ f64(v).transpose(0, 3, 2, 1, 4)
    ctx = ctx.transpose(0, 3, 2, 1, 4).reshape(B * T * S, C)
    return (mxq(ctx, 1, "e4m3") @ unpack4(W_out_words, W_out_scales)).reshape(B, T * S, CO)

@@ -1,0 +1,175 @@
+from contextlib import ExitStack
+
+import concourse.mybir as mybir
+from concourse.masks import make_identity
+
+BF16 = mybir.dt.bfloat16
+F32 = mybir.dt.float32
+I32 = mybir.dt.int32
+U32 = mybir.dt.uint32
+U8 = mybir.dt.uint8
+FP8X4 = mybir.dt.float8_e4m3fn_x4
+FP4X4 = mybir.dt.float4_e2m1fn_x4
+
+B, T, S, H, HD = 2, 128, 16, 8, 128
+C = H * HD
+CO = 1024
+P = 128
+K_PASS = 4 * P
+G = C // K_PASS
+N_MX = 512
+
+S_RUN = 2
+ROUNDS = B * S // S_RUN
+T_HI = P // (H * S_RUN)
+T_LO = T // T_HI
+TL_BANK = 8
+LOAD_BUFS = 4
+
+FLOPS = 2 * B * T * S * C * CO + 2 * B * H * S * T * T * HD
+
+
+def tile_localtemporalattention_pa_kernel(tc, attn, v, W_out_words, W_out_scales, out):
+    nc = tc.nc
+    with ExitStack() as stack:
+        const = stack.enter_context(tc.tile_pool(name="const", bufs=1))
+        loads = stack.enter_context(tc.tile_pool(name="loads", bufs=LOAD_BUFS))
+        work = stack.enter_context(tc.tile_pool(name="work", bufs=2))
+        stage = stack.enter_context(tc.tile_pool(name="stage", bufs=4))
+        psum = stack.enter_context(tc.psum_pool(name="psum", bufs=1))
+        stack.enter_context(tc.manual_schedule())
+
+        attn_sb, v_sb, attnT, ctx_words, grouped, codes, code_scales = {}, {}, {}, {}, {}, {}, {}
+
+        def batch_and_location(r):
+            return divmod(r * S_RUN, S)
+
+        def load_attn(r):
+            b, s0 = batch_and_location(r)
+            attn_sb[r] = loads.tile([P, T_LO * T], BF16, name="attn_sb")
+            nc.sync.dma_start(
+                out=attn_sb[r][:],
+                in_=attn[b, :, s0 : s0 + S_RUN].rearrange("h s (th tl) u -> (s th) h (tl u)", tl=T_LO),
+            )
+
+        def load_v(r):
+            b, s0 = batch_and_location(r)
+            v_sb[r] = loads.tile([P, S_RUN, C], BF16, name="v_sb")
+            nc.sync.dma_start(out=v_sb[r][:], in_=v[b, :, s0 : s0 + S_RUN].rearrange("u s h d -> u s (h d)"))
+
+        def load_weight():
+            for quadrant in range(4):
+                rows = slice(4 * quadrant, 4 * quadrant + 4)
+                nc.sync.dma_start(
+                    out=w_planes[32 * quadrant : 32 * quadrant + 4].bitcast(I32),
+                    in_=W_out_scales[:, rows, :].rearrange("g q n -> q g n").bitcast(I32),
+                )
+            for g in range(G):
+                nc.sync.dma_start(out=w_words[:, g, :].bitcast(I32), in_=W_out_words[g].bitcast(I32))
+
+        def transpose_attn(r):
+            attnT[r] = work.tile([P, H * S_RUN, T_LO, T_HI], BF16, name="attnT")
+            for first in range(0, T_LO, TL_BANK):
+                attnT_ps = psum.tile([P, TL_BANK, P], BF16, name="attnT_ps", bufs=2)
+                for i in range(TL_BANK):
+                    tl = first + i
+                    nc.tensor.transpose(
+                        out=attnT_ps[:, i, :], in_=attn_sb[r][:, tl * T : (tl + 1) * T], identity=by_head[:]
+                    )
+                nc.scalar.copy(
+                    out=attnT[r][:].bitcast(F32)[:, :, first : first + TL_BANK, :],
+                    in_=attnT_ps[:].bitcast(F32).rearrange("u tl (hs w) -> u hs tl w", w=T_HI // 2),
+                )
+
+        def mix_frames(r, sl):
+            if sl == 0:
+                ctx_words[r] = work.tile([P, S_RUN, G, 2, P], F32, name="ctx_words")
+            ctx_ps = psum.tile([P, C], BF16, name="ctx_ps", bufs=2)
+            for h in range(H):
+                nc.tensor.matmul(
+                    out=ctx_ps[:, h * HD : (h + 1) * HD],
+                    lhsT=attnT[r][:, h * S_RUN + sl].rearrange("u tl th -> u (tl th)"),
+                    rhs=v_sb[r][:, sl, h * HD : (h + 1) * HD],
+                    start=True,
+                    stop=True,
+                )
+            nc.vector.tensor_copy(
+                out=ctx_words[r][:, sl], in_=ctx_ps[:].bitcast(F32).rearrange("m (g p w) -> m g w p", g=G, w=2)
+            )
+
+        def transpose_ctx(r, sl):
+            if sl == 0:
+                grouped[r] = work.tile([P, S_RUN, G, P, 4], BF16, name="grouped", align_bytes=64)
+            ctxT_ps = psum.tile([P, G, 2, P], F32, name="ctxT_ps", bufs=1)
+            for g in range(G):
+                for w in range(2):
+                    nc.tensor.transpose(out=ctxT_ps[:, g, w, :], in_=ctx_words[r][:, sl, g, w, :], identity=ident[:])
+            nc.vector.tensor_copy(
+                out=grouped[r][:, sl].bitcast(F32), in_=ctxT_ps[:].rearrange("p g w m -> p g m w")
+            )
+
+        def quantise(r):
+            codes[r] = work.tile([P, S_RUN * G * P], U32, name="codes", align_bytes=64)
+            code_scales[r] = work.tile([P, S_RUN * G * P], U8, name="code_scales", align_bytes=64)
+            nc.vector.quantize_mx(
+                out=codes[r][:].bitcast(FP8X4),
+                scales=code_scales[r][:],
+                in_=grouped[r][:].rearrange("p s g m j -> p (s g m j)"),
+            )
+
+        def project(r, sl):
+            b, s0 = batch_and_location(r)
+            out_sb = stage.tile([P, CO], F32, name="out_sb")
+            for n0 in range(0, CO, N_MX):
+                acc = psum.tile([P, N_MX], F32, name="acc", bufs=3)
+                for g in range(G):
+                    rows = slice((sl * G + g) * P, (sl * G + g + 1) * P)
+                    nc.tensor.matmul_mx(
+                        out=acc[:],
+                        lhsT=codes[r][:, rows].bitcast(FP8X4),
+                        lhsT_scale=code_scales[r][:, rows],
+                        rhs=w_words[:, g, 2 * n0 : 2 * (n0 + N_MX)].bitcast(FP4X4),
+                        rhs_scale=w_planes[:, g, n0 : n0 + N_MX],
+                        start=(g == 0),
+                        stop=(g == G - 1),
+                    )
+                nc.scalar.copy(out=out_sb[:, n0 : n0 + N_MX], in_=acc[:])
+            rows_of_location = out[b].rearrange("(th tl s) c -> tl th s c", th=T_HI, tl=T_LO)[:, :, s0 + sl, :]
+            nc.sync.dma_start(out=rows_of_location, in_=out_sb[:])
+
+        w_words = const.tile([P, G, 2 * CO], U8, name="w_words", align_bytes=64)
+        w_planes = const.tile([P, G, CO], U8, name="w_planes", align_bytes=64)
+        nc.vector.memset(w_planes[:].bitcast(I32), 0)
+        for r in range(LOAD_BUFS):
+            load_attn(r)
+            load_v(r)
+            if r == 1:
+                load_weight()
+        ident = const.tile([P, P], F32, name="ident")
+        make_identity(nc, ident[:])
+        by_head = const.tile([P, P], BF16, name="by_head")
+        nc.vector.tensor_copy(
+            out=by_head[:].rearrange("i (h x) -> i h x", h=H), in_=ident[:].rearrange("i (x h) -> i h x", h=H)
+        )
+
+        for p in range(-1, ROUNDS + 2):
+            mixes, flips, projects = 0 <= p < ROUNDS, 0 <= p - 1 < ROUNDS, 0 <= p - 2 < ROUNDS
+            if mixes:
+                mix_frames(p, 0)
+            if flips:
+                transpose_ctx(p - 1, 0)
+            if p + 1 < ROUNDS:
+                transpose_attn(p + 1)
+            if p + 1 + LOAD_BUFS < ROUNDS:
+                load_attn(p + 1 + LOAD_BUFS)
+            if flips:
+                transpose_ctx(p - 1, 1)
+            if mixes:
+                mix_frames(p, 1)
+            if mixes and p + LOAD_BUFS < ROUNDS:
+                load_v(p + LOAD_BUFS)
+            if flips:
+                quantise(p - 1)
+            if projects:
+                for sl in range(S_RUN):
+                    project(p - 2, sl)

@@ -24,7 +24,10 @@ ROUNDS = B * S // S_RUN
 T_HI = P // (H * S_RUN)
 T_LO = T // T_HI
 TL_BANK = 8
-LOAD_BUFS = 4
+PSUM_BANKS = 8
+LOAD_BUFS = 6
+
+assert TL_BANK == H and S_RUN * TL_BANK == T_LO
 
 FLOPS = 2 * B * T * S * C * CO + 2 * B * H * S * T * T * HD
 
@@ -36,7 +39,7 @@ def tile_localtemporalattention_pa_kernel(tc, attn, v, W_out_words, W_out_scales
         loads = stack.enter_context(tc.tile_pool(name="loads", bufs=LOAD_BUFS))
         work = stack.enter_context(tc.tile_pool(name="work", bufs=2))
         stage = stack.enter_context(tc.tile_pool(name="stage", bufs=4))
-        psum = stack.enter_context(tc.psum_pool(name="psum", bufs=1))
+        psum = stack.enter_context(tc.psum_pool(name="psum", bufs=PSUM_BANKS))
         stack.enter_context(tc.manual_schedule())
 
         attn_sb, v_sb, attnT, ctx_words, grouped, codes, code_scales = {}, {}, {}, {}, {}, {}, {}
@@ -67,40 +70,45 @@ def tile_localtemporalattention_pa_kernel(tc, attn, v, W_out_words, W_out_scales
             for g in range(G):
                 nc.sync.dma_start(out=w_words[:, g, :].bitcast(I32), in_=W_out_words[g].bitcast(I32))
 
-        def transpose_attn(r):
-            attnT[r] = work.tile([P, H * S_RUN, T_LO, T_HI], BF16, name="attnT")
-            for first in range(0, T_LO, TL_BANK):
-                attnT_ps = psum.tile([P, TL_BANK, P], BF16, name="attnT_ps", bufs=2)
-                for i in range(TL_BANK):
-                    tl = first + i
-                    nc.tensor.transpose(
-                        out=attnT_ps[:, i, :], in_=attn_sb[r][:, tl * T : (tl + 1) * T], identity=by_head[:]
+        def mix_and_transpose(r, sl):
+            mixes, turns = 0 <= r < ROUNDS, r + 1 < ROUNDS
+            if mixes:
+                ctx_ps = psum.tile([P, C], BF16, name="ctx_ps", tag="bank")
+            if turns:
+                attnT_ps = psum.tile([P, TL_BANK, P], BF16, name="attnT_ps", tag="bank")
+            for i in range(H):
+                if mixes:
+                    nc.tensor.matmul(
+                        out=ctx_ps[:, i * HD : (i + 1) * HD],
+                        lhsT=attnT[r][:, i * S_RUN + sl].rearrange("u tl th -> u (tl th)"),
+                        rhs=v_sb[r][:, sl, i * HD : (i + 1) * HD],
+                        start=True,
+                        stop=True,
                     )
+                if turns:
+                    tl = sl * TL_BANK + i
+                    nc.tensor.transpose(
+                        out=attnT_ps[:, i, :], in_=attn_sb[r + 1][:, tl * T : (tl + 1) * T], identity=by_head[:]
+                    )
+            if mixes:
+                if sl == 0:
+                    ctx_words[r] = work.tile([P, S_RUN, G, 2, P], F32, name="ctx_words")
+                nc.vector.tensor_copy(
+                    out=ctx_words[r][:, sl],
+                    in_=ctx_ps[:].bitcast(F32).rearrange("m (g p w) -> m g w p", g=G, w=2),
+                )
+            if turns:
+                if sl == 0:
+                    attnT[r + 1] = work.tile([P, H * S_RUN, T_LO, T_HI], BF16, name="attnT")
                 nc.scalar.copy(
-                    out=attnT[r][:].bitcast(F32)[:, :, first : first + TL_BANK, :],
+                    out=attnT[r + 1][:].bitcast(F32)[:, :, sl * TL_BANK : (sl + 1) * TL_BANK, :],
                     in_=attnT_ps[:].bitcast(F32).rearrange("u tl (hs w) -> u hs tl w", w=T_HI // 2),
                 )
-
-        def mix_frames(r, sl):
-            if sl == 0:
-                ctx_words[r] = work.tile([P, S_RUN, G, 2, P], F32, name="ctx_words")
-            ctx_ps = psum.tile([P, C], BF16, name="ctx_ps", bufs=2)
-            for h in range(H):
-                nc.tensor.matmul(
-                    out=ctx_ps[:, h * HD : (h + 1) * HD],
-                    lhsT=attnT[r][:, h * S_RUN + sl].rearrange("u tl th -> u (tl th)"),
-                    rhs=v_sb[r][:, sl, h * HD : (h + 1) * HD],
-                    start=True,
-                    stop=True,
-                )
-            nc.vector.tensor_copy(
-                out=ctx_words[r][:, sl], in_=ctx_ps[:].bitcast(F32).rearrange("m (g p w) -> m g w p", g=G, w=2)
-            )
 
         def transpose_ctx(r, sl):
             if sl == 0:
                 grouped[r] = work.tile([P, S_RUN, G, P, 4], BF16, name="grouped", align_bytes=64)
-            ctxT_ps = psum.tile([P, G, 2, P], F32, name="ctxT_ps", bufs=1)
+            ctxT_ps = psum.tile([P, G, 2, P], F32, name="ctxT_ps", tag="bank")
             for g in range(G):
                 for w in range(2):
                     nc.tensor.transpose(out=ctxT_ps[:, g, w, :], in_=ctx_words[r][:, sl, g, w, :], identity=ident[:])
@@ -121,7 +129,7 @@ def tile_localtemporalattention_pa_kernel(tc, attn, v, W_out_words, W_out_scales
             b, s0 = batch_and_location(r)
             out_sb = stage.tile([P, CO], F32, name="out_sb")
             for n0 in range(0, CO, N_MX):
-                acc = psum.tile([P, N_MX], F32, name="acc", bufs=3)
+                acc = psum.tile([P, N_MX], F32, name="acc", tag="bank")
                 for g in range(G):
                     rows = slice((sl * G + g) * P, (sl * G + g + 1) * P)
                     nc.tensor.matmul_mx(
@@ -153,23 +161,16 @@ def tile_localtemporalattention_pa_kernel(tc, attn, v, W_out_words, W_out_scales
         )
 
         for p in range(-1, ROUNDS + 2):
-            mixes, flips, projects = 0 <= p < ROUNDS, 0 <= p - 1 < ROUNDS, 0 <= p - 2 < ROUNDS
-            if mixes:
-                mix_frames(p, 0)
-            if flips:
-                transpose_ctx(p - 1, 0)
-            if p + 1 < ROUNDS:
-                transpose_attn(p + 1)
+            for sl in range(S_RUN):
+                mix_and_transpose(p, sl)
             if p + 1 + LOAD_BUFS < ROUNDS:
                 load_attn(p + 1 + LOAD_BUFS)
-            if flips:
-                transpose_ctx(p - 1, 1)
-            if mixes:
-                mix_frames(p, 1)
-            if mixes and p + LOAD_BUFS < ROUNDS:
+            if 0 <= p and p + LOAD_BUFS < ROUNDS:
                 load_v(p + LOAD_BUFS)
-            if flips:
+            if 0 <= p - 1 < ROUNDS:
+                for sl in range(S_RUN):
+                    transpose_ctx(p - 1, sl)
                 quantise(p - 1)
-            if projects:
+            if 0 <= p - 2 < ROUNDS:
                 for sl in range(S_RUN):
                     project(p - 2, sl)

@@ -25,7 +25,7 @@ T_HI = P // (H * S_RUN)
 T_LO = T // T_HI
 TL_BANK = 8
 PSUM_BANKS = 8
-LOAD_BUFS = 6
+OUT_BUFS = 8
 
 assert TL_BANK == H and S_RUN * TL_BANK == T_LO
 
@@ -36,9 +36,9 @@ def tile_localtemporalattention_pa_kernel(tc, attn, v, W_out_words, W_out_scales
     nc = tc.nc
     with ExitStack() as stack:
         const = stack.enter_context(tc.tile_pool(name="const", bufs=1))
-        loads = stack.enter_context(tc.tile_pool(name="loads", bufs=LOAD_BUFS))
+        loads = stack.enter_context(tc.tile_pool(name="loads", bufs=ROUNDS))
         work = stack.enter_context(tc.tile_pool(name="work", bufs=2))
-        stage = stack.enter_context(tc.tile_pool(name="stage", bufs=4))
+        stage = stack.enter_context(tc.tile_pool(name="stage", bufs=OUT_BUFS))
         psum = stack.enter_context(tc.psum_pool(name="psum", bufs=PSUM_BANKS))
         stack.enter_context(tc.manual_schedule())
 
@@ -148,7 +148,7 @@ def tile_localtemporalattention_pa_kernel(tc, attn, v, W_out_words, W_out_scales
         w_words = const.tile([P, G, 2 * CO], U8, name="w_words", align_bytes=64)
         w_planes = const.tile([P, G, CO], U8, name="w_planes", align_bytes=64)
         nc.vector.memset(w_planes[:].bitcast(I32), 0)
-        for r in range(LOAD_BUFS):
+        for r in range(ROUNDS):
             load_attn(r)
             load_v(r)
             if r == 1:
@@ -163,10 +163,6 @@ def tile_localtemporalattention_pa_kernel(tc, attn, v, W_out_words, W_out_scales
         for p in range(-1, ROUNDS + 2):
             for sl in range(S_RUN):
                 mix_and_transpose(p, sl)
-            if p + 1 + LOAD_BUFS < ROUNDS:
-                load_attn(p + 1 + LOAD_BUFS)
-            if 0 <= p and p + LOAD_BUFS < ROUNDS:
-                load_v(p + LOAD_BUFS)
             if 0 <= p - 1 < ROUNDS:
                 for sl in range(S_RUN):
                     transpose_ctx(p - 1, sl)

@@ -19,13 +19,14 @@ K_PASS = 4 * P
 G = C // K_PASS
 N_MX = 512
 
-S_RUN = 2
+S_RUN = 4
+S_STORE = 2
 ROUNDS = B * S // S_RUN
 T_HI = P // (H * S_RUN)
 T_LO = T // T_HI
 TL_BANK = 8
 PSUM_BANKS = 8
-OUT_BUFS = 8
+LOAD_BUFS = 3
 
 assert TL_BANK == H and S_RUN * TL_BANK == T_LO
 
@@ -36,9 +37,9 @@ def tile_localtemporalattention_pa_kernel(tc, attn, v, W_out_words, W_out_scales
     nc = tc.nc
     with ExitStack() as stack:
         const = stack.enter_context(tc.tile_pool(name="const", bufs=1))
-        loads = stack.enter_context(tc.tile_pool(name="loads", bufs=ROUNDS))
+        loads = stack.enter_context(tc.tile_pool(name="loads", bufs=LOAD_BUFS))
         work = stack.enter_context(tc.tile_pool(name="work", bufs=2))
-        stage = stack.enter_context(tc.tile_pool(name="stage", bufs=OUT_BUFS))
+        stage = stack.enter_context(tc.tile_pool(name="stage", bufs=4))
         psum = stack.enter_context(tc.psum_pool(name="psum", bufs=PSUM_BANKS))
         stack.enter_context(tc.manual_schedule())
 
@@ -125,33 +126,35 @@ def tile_localtemporalattention_pa_kernel(tc, attn, v, W_out_words, W_out_scales
                 in_=grouped[r][:].rearrange("p s g m j -> p (s g m j)"),
             )
 
-        def project(r, sl):
+        def project(r, first):
             b, s0 = batch_and_location(r)
-            out_sb = stage.tile([P, CO], F32, name="out_sb")
-            for n0 in range(0, CO, N_MX):
-                acc = psum.tile([P, N_MX], F32, name="acc", tag="bank")
-                for g in range(G):
-                    rows = slice((sl * G + g) * P, (sl * G + g + 1) * P)
-                    nc.tensor.matmul_mx(
-                        out=acc[:],
-                        lhsT=codes[r][:, rows].bitcast(FP8X4),
-                        lhsT_scale=code_scales[r][:, rows],
-                        rhs=w_words[:, g, 2 * n0 : 2 * (n0 + N_MX)].bitcast(FP4X4),
-                        rhs_scale=w_planes[:, g, n0 : n0 + N_MX],
-                        start=(g == 0),
-                        stop=(g == G - 1),
-                    )
-                nc.scalar.copy(out=out_sb[:, n0 : n0 + N_MX], in_=acc[:])
-            rows_of_location = out[b].rearrange("(th tl s) c -> tl th s c", th=T_HI, tl=T_LO)[:, :, s0 + sl, :]
-            nc.sync.dma_start(out=rows_of_location, in_=out_sb[:])
+            out_sb = stage.tile([P, S_STORE, CO], F32, name="out_sb")
+            for i in range(S_STORE):
+                for n0 in range(0, CO, N_MX):
+                    acc = psum.tile([P, N_MX], F32, name="acc", tag="bank")
+                    for g in range(G):
+                        rows = slice(((first + i) * G + g) * P, ((first + i) * G + g + 1) * P)
+                        nc.tensor.matmul_mx(
+                            out=acc[:],
+                            lhsT=codes[r][:, rows].bitcast(FP8X4),
+                            lhsT_scale=code_scales[r][:, rows],
+                            rhs=w_words[:, g, 2 * n0 : 2 * (n0 + N_MX)].bitcast(FP4X4),
+                            rhs_scale=w_planes[:, g, n0 : n0 + N_MX],
+                            start=(g == 0),
+                            stop=(g == G - 1),
+                        )
+                    nc.scalar.copy(out=out_sb[:, i, n0 : n0 + N_MX], in_=acc[:])
+            s = s0 + first
+            rows_of_t = out[b].rearrange("(th tl s) c -> tl th (s c)", th=T_HI, tl=T_LO)
+            nc.sync.dma_start(out=rows_of_t[:, :, s * CO : (s + S_STORE) * CO], in_=out_sb[:])
 
         w_words = const.tile([P, G, 2 * CO], U8, name="w_words", align_bytes=64)
         w_planes = const.tile([P, G, CO], U8, name="w_planes", align_bytes=64)
         nc.vector.memset(w_planes[:].bitcast(I32), 0)
-        for r in range(ROUNDS):
+        for r in range(LOAD_BUFS):
             load_attn(r)
             load_v(r)
-            if r == 1:
+            if r == 0:
                 load_weight()
         ident = const.tile([P, P], F32, name="ident")
         make_identity(nc, ident[:])
@@ -163,10 +166,14 @@ def tile_localtemporalattention_pa_kernel(tc, attn, v, W_out_words, W_out_scales
         for p in range(-1, ROUNDS + 2):
             for sl in range(S_RUN):
                 mix_and_transpose(p, sl)
+            if p + 1 + LOAD_BUFS < ROUNDS:
+                load_attn(p + 1 + LOAD_BUFS)
+            if 0 <= p and p + LOAD_BUFS < ROUNDS:
+                load_v(p + LOAD_BUFS)
             if 0 <= p - 1 < ROUNDS:
                 for sl in range(S_RUN):
                     transpose_ctx(p - 1, sl)
                 quantise(p - 1)
             if 0 <= p - 2 < ROUNDS:
-                for sl in range(S_RUN):
-                    project(p - 2, sl)
+                for first in range(0, S_RUN, S_STORE):
+                    project(p - 2, first)

@@ -26,7 +26,8 @@ T_HI = P // (H * S_RUN)
 T_LO = T // T_HI
 TL_BANK = 8
 PSUM_BANKS = 8
-LOAD_BUFS = 3
+LOAD_BUFS = 5
+FINE_ROUNDS = 4
 
 assert TL_BANK == H and S_RUN * TL_BANK == T_LO
 
@@ -39,7 +40,7 @@ def tile_localtemporalattention_pa_kernel(tc, attn, v, W_out_words, W_out_scales
         const = stack.enter_context(tc.tile_pool(name="const", bufs=1))
         loads = stack.enter_context(tc.tile_pool(name="loads", bufs=LOAD_BUFS))
         work = stack.enter_context(tc.tile_pool(name="work", bufs=2))
-        stage = stack.enter_context(tc.tile_pool(name="stage", bufs=4))
+        stage = stack.enter_context(tc.tile_pool(name="stage", bufs=6))
         psum = stack.enter_context(tc.psum_pool(name="psum", bufs=PSUM_BANKS))
         stack.enter_context(tc.manual_schedule())
 
@@ -48,18 +49,32 @@ def tile_localtemporalattention_pa_kernel(tc, attn, v, W_out_words, W_out_scales
         def batch_and_location(r):
             return divmod(r * S_RUN, S)
 
-        def load_attn(r):
+        def load_attn(r, quarters):
             b, s0 = batch_and_location(r)
-            attn_sb[r] = loads.tile([P, T_LO * T], BF16, name="attn_sb")
+            if r not in attn_sb:
+                attn_sb[r] = loads.tile([P, T_LO * T], BF16, name="attn_sb")
+            cols = slice(quarters[0] * TL_BANK * T, (quarters[-1] + 1) * TL_BANK * T)
             nc.sync.dma_start(
-                out=attn_sb[r][:],
-                in_=attn[b, :, s0 : s0 + S_RUN].rearrange("h s (th tl) u -> (s th) h (tl u)", tl=T_LO),
+                out=attn_sb[r][:, cols],
+                in_=attn[b, :, s0 : s0 + S_RUN].rearrange("h s (th tl) u -> (s th) h (tl u)", tl=T_LO)[:, :, cols],
             )
 
-        def load_v(r):
+        def load_v(r, locations):
             b, s0 = batch_and_location(r)
-            v_sb[r] = loads.tile([P, S_RUN, C], BF16, name="v_sb")
-            nc.sync.dma_start(out=v_sb[r][:], in_=v[b, :, s0 : s0 + S_RUN].rearrange("u s h d -> u s (h d)"))
+            if r not in v_sb:
+                v_sb[r] = loads.tile([P, S_RUN, C], BF16, name="v_sb")
+            first, last = locations[0], locations[-1] + 1
+            nc.sync.dma_start(
+                out=v_sb[r][:, first:last], in_=v[b, :, s0 + first : s0 + last].rearrange("u s h d -> u s (h d)")
+            )
+
+        def load_pair(r):
+            whole = list(range(S_RUN))
+            for part in [[q] for q in whole] if r < FINE_ROUNDS else [whole]:
+                if 0 <= r - 1 < ROUNDS:
+                    load_v(r - 1, part)
+                if r < ROUNDS:
+                    load_attn(r, part)
 
         def load_weight():
             for quadrant in range(4):
@@ -113,9 +128,7 @@ def tile_localtemporalattention_pa_kernel(tc, attn, v, W_out_words, W_out_scales
             for g in range(G):
                 for w in range(2):
                     nc.tensor.transpose(out=ctxT_ps[:, g, w, :], in_=ctx_words[r][:, sl, g, w, :], identity=ident[:])
-            nc.vector.tensor_copy(
-                out=grouped[r][:, sl].bitcast(F32), in_=ctxT_ps[:].rearrange("p g w m -> p g m w")
-            )
+            nc.scalar.copy(out=grouped[r][:, sl].bitcast(F32), in_=ctxT_ps[:].rearrange("p g w m -> p g m w"))
 
         def quantise(r):
             codes[r] = work.tile([P, S_RUN * G * P], U32, name="codes", align_bytes=64)
@@ -126,10 +139,10 @@ def tile_localtemporalattention_pa_kernel(tc, attn, v, W_out_words, W_out_scales
                 in_=grouped[r][:].rearrange("p s g m j -> p (s g m j)"),
             )
 
-        def project(r, first):
+        def project(r, first, count):
             b, s0 = batch_and_location(r)
             out_sb = stage.tile([P, S_STORE, CO], F32, name="out_sb")
-            for i in range(S_STORE):
+            for i in range(count):
                 for n0 in range(0, CO, N_MX):
                     acc = psum.tile([P, N_MX], F32, name="acc", tag="bank")
                     for g in range(G):
@@ -143,18 +156,20 @@ def tile_localtemporalattention_pa_kernel(tc, attn, v, W_out_words, W_out_scales
                             start=(g == 0),
                             stop=(g == G - 1),
                         )
-                    nc.scalar.copy(out=out_sb[:, i, n0 : n0 + N_MX], in_=acc[:])
+                    if n0 == 0:
+                        nc.scalar.copy(out=out_sb[:, i, n0 : n0 + N_MX], in_=acc[:])
+                    else:
+                        nc.vector.tensor_copy(out=out_sb[:, i, n0 : n0 + N_MX], in_=acc[:])
             s = s0 + first
             rows_of_t = out[b].rearrange("(th tl s) c -> tl th (s c)", th=T_HI, tl=T_LO)
-            nc.sync.dma_start(out=rows_of_t[:, :, s * CO : (s + S_STORE) * CO], in_=out_sb[:])
+            nc.sync.dma_start(out=rows_of_t[:, :, s * CO : (s + count) * CO], in_=out_sb[:, :count])
 
         w_words = const.tile([P, G, 2 * CO], U8, name="w_words", align_bytes=64)
         w_planes = const.tile([P, G, CO], U8, name="w_planes", align_bytes=64)
         nc.vector.memset(w_planes[:].bitcast(I32), 0)
         for r in range(LOAD_BUFS):
-            load_attn(r)
-            load_v(r)
-            if r == 0:
+            load_pair(r)
+            if r == FINE_ROUNDS - 1:
                 load_weight()
         ident = const.tile([P, P], F32, name="ident")
         make_identity(nc, ident[:])
@@ -166,14 +181,13 @@ def tile_localtemporalattention_pa_kernel(tc, attn, v, W_out_words, W_out_scales
         for p in range(-1, ROUNDS + 2):
             for sl in range(S_RUN):
                 mix_and_transpose(p, sl)
-            if p + 1 + LOAD_BUFS < ROUNDS:
-                load_attn(p + 1 + LOAD_BUFS)
-            if 0 <= p and p + LOAD_BUFS < ROUNDS:
-                load_v(p + LOAD_BUFS)
+            if p + LOAD_BUFS < ROUNDS:
+                load_pair(p + 1 + LOAD_BUFS)
             if 0 <= p - 1 < ROUNDS:
                 for sl in range(S_RUN):
                     transpose_ctx(p - 1, sl)
                 quantise(p - 1)
             if 0 <= p - 2 < ROUNDS:
-                for first in range(0, S_RUN, S_STORE):
-                    project(p - 2, first)
+                step = S_STORE if p - 2 < ROUNDS - 1 else 1
+                for first in range(0, S_RUN, step):
+                    project(p - 2, first, step)

@@ -162,7 +162,7 @@ def tile_localtemporalattention_pa_kernel(tc, attn, v, W_out_words, W_out_scales
                         nc.vector.tensor_copy(out=out_sb[:, i, n0 : n0 + N_MX], in_=acc[:])
             s = s0 + first
             rows_of_t = out[b].rearrange("(th tl s) c -> tl th (s c)", th=T_HI, tl=T_LO)
-            nc.sync.dma_start(out=rows_of_t[:, :, s * CO : (s + count) * CO], in_=out_sb[:, :count])
+            nc.gpsimd.dma_start(out=rows_of_t[:, :, s * CO : (s + count) * CO], in_=out_sb[:, :count])
 
         w_words = const.tile([P, G, 2 * CO], U8, name="w_words", align_bytes=64)
         w_planes = const.tile([P, G, CO], U8, name="w_planes", align_bytes=64)

@@ -162,14 +162,15 @@ def tile_localtemporalattention_pa_kernel(tc, attn, v, W_out_words, W_out_scales
                         nc.vector.tensor_copy(out=out_sb[:, i, n0 : n0 + N_MX], in_=acc[:])
             s = s0 + first
             rows_of_t = out[b].rearrange("(th tl s) c -> tl th (s c)", th=T_HI, tl=T_LO)
-            nc.gpsimd.dma_start(out=rows_of_t[:, :, s * CO : (s + count) * CO], in_=out_sb[:, :count])
+            queue = nc.gpsimd if r < ROUNDS - 1 else nc.sync
+            queue.dma_start(out=rows_of_t[:, :, s * CO : (s + count) * CO], in_=out_sb[:, :count])
 
         w_words = const.tile([P, G, 2 * CO], U8, name="w_words", align_bytes=64)
         w_planes = const.tile([P, G, CO], U8, name="w_planes", align_bytes=64)
         nc.vector.memset(w_planes[:].bitcast(I32), 0)
         for r in range(LOAD_BUFS):
             load_pair(r)
-            if r == FINE_ROUNDS - 1:
+            if r == 2:
                 load_weight()
         ident = const.tile([P, P], F32, name="ident")
         make_identity(nc, ident[:])
@@ -178,16 +179,17 @@ def tile_localtemporalattention_pa_kernel(tc, attn, v, W_out_words, W_out_scales
             out=by_head[:].rearrange("i (h x) -> i h x", h=H), in_=ident[:].rearrange("i (x h) -> i h x", h=H)
         )
 
-        for p in range(-1, ROUNDS + 2):
+        for p in range(-1, ROUNDS + 1):
             for sl in range(S_RUN):
                 mix_and_transpose(p, sl)
             if p + LOAD_BUFS < ROUNDS:
                 load_pair(p + 1 + LOAD_BUFS)
-            if 0 <= p - 1 < ROUNDS:
+            if 0 <= p < ROUNDS:
                 for sl in range(S_RUN):
-                    transpose_ctx(p - 1, sl)
-                quantise(p - 1)
-            if 0 <= p - 2 < ROUNDS:
-                step = S_STORE if p - 2 < ROUNDS - 1 else 1
-                for first in range(0, S_RUN, step):
-                    project(p - 2, first, step)
+                    transpose_ctx(p, sl)
+            step = S_STORE if p - 1 < ROUNDS - 1 else 1
+            for first in range(0, S_RUN, step):
+                if first == S_RUN // 2 and 0 <= p < ROUNDS:
+                    quantise(p)
+                if 0 <= p - 1 < ROUNDS:
+                    project(p - 1, first, step)

@@ -44,7 +44,7 @@ def tile_localtemporalattention_pa_kernel(tc, attn, v, W_out_words, W_out_scales
         psum = stack.enter_context(tc.psum_pool(name="psum", bufs=PSUM_BANKS))
         stack.enter_context(tc.manual_schedule())
 
-        attn_sb, v_sb, attnT, ctx_words, grouped, codes, code_scales = {}, {}, {}, {}, {}, {}, {}
+        attn_sb, v_sb, attnT, ctx_words, grouped, codes, code_scales, out_sb = {}, {}, {}, {}, {}, {}, {}, {}
 
         def batch_and_location(r):
             return divmod(r * S_RUN, S)
@@ -70,7 +70,7 @@ def tile_localtemporalattention_pa_kernel(tc, attn, v, W_out_words, W_out_scales
 
         def load_pair(r):
             whole = list(range(S_RUN))
-            for part in [[q] for q in whole] if r < FINE_ROUNDS else [whole]:
+            for part in [[q] for q in whole] if r < FINE_ROUNDS or r == ROUNDS else [whole]:
                 if 0 <= r - 1 < ROUNDS:
                     load_v(r - 1, part)
                 if r < ROUNDS:
@@ -130,47 +130,51 @@ def tile_localtemporalattention_pa_kernel(tc, attn, v, W_out_words, W_out_scales
                     nc.tensor.transpose(out=ctxT_ps[:, g, w, :], in_=ctx_words[r][:, sl, g, w, :], identity=ident[:])
             nc.scalar.copy(out=grouped[r][:, sl].bitcast(F32), in_=ctxT_ps[:].rearrange("p g w m -> p g m w"))
 
-        def quantise(r):
-            codes[r] = work.tile([P, S_RUN * G * P], U32, name="codes", align_bytes=64)
-            code_scales[r] = work.tile([P, S_RUN * G * P], U8, name="code_scales", align_bytes=64)
+        def quantise(r, first):
+            if first == 0:
+                codes[r] = work.tile([P, S_RUN * G * P], U32, name="codes", align_bytes=64)
+                code_scales[r] = work.tile([P, S_RUN * G * P], U8, name="code_scales", align_bytes=64)
+            cols = slice(first * G * P, (first + S_STORE) * G * P)
             nc.vector.quantize_mx(
-                out=codes[r][:].bitcast(FP8X4),
-                scales=code_scales[r][:],
-                in_=grouped[r][:].rearrange("p s g m j -> p (s g m j)"),
+                out=codes[r][:, cols].bitcast(FP8X4),
+                scales=code_scales[r][:, cols],
+                in_=grouped[r][:, first : first + S_STORE].rearrange("p s g m j -> p (s g m j)"),
             )
 
-        def project(r, first, count):
+        def project(r, sl, width):
             b, s0 = batch_and_location(r)
-            out_sb = stage.tile([P, S_STORE, CO], F32, name="out_sb")
-            for i in range(count):
-                for n0 in range(0, CO, N_MX):
-                    acc = psum.tile([P, N_MX], F32, name="acc", tag="bank")
-                    for g in range(G):
-                        rows = slice(((first + i) * G + g) * P, ((first + i) * G + g + 1) * P)
-                        nc.tensor.matmul_mx(
-                            out=acc[:],
-                            lhsT=codes[r][:, rows].bitcast(FP8X4),
-                            lhsT_scale=code_scales[r][:, rows],
-                            rhs=w_words[:, g, 2 * n0 : 2 * (n0 + N_MX)].bitcast(FP4X4),
-                            rhs_scale=w_planes[:, g, n0 : n0 + N_MX],
-                            start=(g == 0),
-                            stop=(g == G - 1),
-                        )
-                    if n0 == 0:
-                        nc.scalar.copy(out=out_sb[:, i, n0 : n0 + N_MX], in_=acc[:])
-                    else:
-                        nc.vector.tensor_copy(out=out_sb[:, i, n0 : n0 + N_MX], in_=acc[:])
-            s = s0 + first
-            rows_of_t = out[b].rearrange("(th tl s) c -> tl th (s c)", th=T_HI, tl=T_LO)
-            queue = nc.gpsimd if r < ROUNDS - 1 else nc.sync
-            queue.dma_start(out=rows_of_t[:, :, s * CO : (s + count) * CO], in_=out_sb[:, :count])
+            i = sl % width
+            if i == 0:
+                out_sb[r] = stage.tile([P, width, CO], F32, name="out_sb")
+            for n0 in range(0, CO, N_MX):
+                acc = psum.tile([P, N_MX], F32, name="acc", tag="bank")
+                for g in range(G):
+                    rows = slice((sl * G + g) * P, (sl * G + g + 1) * P)
+                    nc.tensor.matmul_mx(
+                        out=acc[:],
+                        lhsT=codes[r][:, rows].bitcast(FP8X4),
+                        lhsT_scale=code_scales[r][:, rows],
+                        rhs=w_words[:, g, 2 * n0 : 2 * (n0 + N_MX)].bitcast(FP4X4),
+                        rhs_scale=w_planes[:, g, n0 : n0 + N_MX],
+                        start=(g == 0),
+                        stop=(g == G - 1),
+                    )
+                if n0 == 0:
+                    nc.scalar.copy(out=out_sb[r][:, i, n0 : n0 + N_MX], in_=acc[:])
+                else:
+                    nc.vector.tensor_copy(out=out_sb[r][:, i, n0 : n0 + N_MX], in_=acc[:])
+            if i == width - 1:
+                s = s0 + sl - i
+                rows_of_t = out[b].rearrange("(th tl s) c -> tl th (s c)", th=T_HI, tl=T_LO)
+                queue = nc.gpsimd if r < ROUNDS - 1 else nc.sync
+                queue.dma_start(out=rows_of_t[:, :, s * CO : (s + width) * CO], in_=out_sb[r][:])
 
         w_words = const.tile([P, G, 2 * CO], U8, name="w_words", align_bytes=64)
         w_planes = const.tile([P, G, CO], U8, name="w_planes", align_bytes=64)
         nc.vector.memset(w_planes[:].bitcast(I32), 0)
         for r in range(LOAD_BUFS):
             load_pair(r)
-            if r == 2:
+            if r == 1:
                 load_weight()
         ident = const.tile([P, P], F32, name="ident")
         make_identity(nc, ident[:])
@@ -179,17 +183,23 @@ def tile_localtemporalattention_pa_kernel(tc, attn, v, W_out_words, W_out_scales
             out=by_head[:].rearrange("i (h x) -> i h x", h=H), in_=ident[:].rearrange("i (x h) -> i h x", h=H)
         )
 
+        half = S_RUN // 2
         for p in range(-1, ROUNDS + 1):
+            here, before = 0 <= p < ROUNDS, 0 <= p - 1 < ROUNDS
             for sl in range(S_RUN):
                 mix_and_transpose(p, sl)
+                if here and sl >= half:
+                    transpose_ctx(p, sl - half)
             if p + LOAD_BUFS < ROUNDS:
                 load_pair(p + 1 + LOAD_BUFS)
-            if 0 <= p < ROUNDS:
-                for sl in range(S_RUN):
+            if here:
+                quantise(p, 0)
+            if before:
+                for sl in range(half, S_RUN):
+                    project(p - 1, sl, S_STORE if p - 1 < ROUNDS - 1 else 1)
+            if here:
+                for sl in range(half, S_RUN):
                     transpose_ctx(p, sl)
-            step = S_STORE if p - 1 < ROUNDS - 1 else 1
-            for first in range(0, S_RUN, step):
-                if first == S_RUN // 2 and 0 <= p < ROUNDS:
-                    quantise(p)
-                if 0 <= p - 1 < ROUNDS:
-                    project(p - 1, first, step)
+                quantise(p, half)
+                for sl in range(half):
+                    project(p, sl, S_STORE if p < ROUNDS - 1 else 1)

@@ -27,6 +27,7 @@ T_LO = T // T_HI
 TL_BANK = 8
 PSUM_BANKS = 8
 LOAD_BUFS = 5
+V_ROUNDS = 2
 FINE_ROUNDS = 4
 
 assert TL_BANK == H and S_RUN * TL_BANK == T_LO
@@ -39,12 +40,13 @@ def tile_localtemporalattention_pa_kernel(tc, attn, v, W_out_words, W_out_scales
     with ExitStack() as stack:
         const = stack.enter_context(tc.tile_pool(name="const", bufs=1))
         loads = stack.enter_context(tc.tile_pool(name="loads", bufs=LOAD_BUFS))
+        v_loads = stack.enter_context(tc.tile_pool(name="v_loads", bufs=3))
         work = stack.enter_context(tc.tile_pool(name="work", bufs=2))
         stage = stack.enter_context(tc.tile_pool(name="stage", bufs=6))
         psum = stack.enter_context(tc.psum_pool(name="psum", bufs=PSUM_BANKS))
         stack.enter_context(tc.manual_schedule())
 
-        attn_sb, v_sb, attnT, ctx_words, grouped, codes, code_scales, out_sb = {}, {}, {}, {}, {}, {}, {}, {}
+        attn_sb, v_sb, v_pairs, attnT, ctx_words, grouped, codes, code_scales, out_sb = {}, {}, {}, {}, {}, {}, {}, {}, {}
 
         def batch_and_location(r):
             return divmod(r * S_RUN, S)
@@ -61,17 +63,24 @@ def tile_localtemporalattention_pa_kernel(tc, attn, v, W_out_words, W_out_scales
 
         def load_v(r, locations):
             b, s0 = batch_and_location(r)
-            if r not in v_sb:
-                v_sb[r] = loads.tile([P, S_RUN, C], BF16, name="v_sb")
+            if r % V_ROUNDS == 0 and r not in v_sb:
+                tile = v_loads.tile([P, V_ROUNDS * S_RUN, C], BF16, name="v_pair")
+                for i in range(V_ROUNDS):
+                    v_sb[r + i] = tile[:, i * S_RUN : (i + 1) * S_RUN]
+                v_pairs[r // V_ROUNDS] = tile
             first, last = locations[0], locations[-1] + 1
+            shift = r % V_ROUNDS * S_RUN
             nc.sync.dma_start(
-                out=v_sb[r][:, first:last], in_=v[b, :, s0 + first : s0 + last].rearrange("u s h d -> u s (h d)")
+                out=v_pairs[r // V_ROUNDS][:, shift + first : shift + last],
+                in_=v[b, :, s0 + first : s0 + last].rearrange("u s h d -> u s (h d)"),
             )
 
         def load_pair(r):
             whole = list(range(S_RUN))
-            for part in [[q] for q in whole] if r < FINE_ROUNDS or r == ROUNDS else [whole]:
-                if 0 <= r - 1 < ROUNDS:
+            if r - 1 >= V_ROUNDS and (r - 1) % V_ROUNDS == 0 and r - 1 < ROUNDS:
+                load_v(r - 1, list(range(V_ROUNDS * S_RUN)))
+            for part in [[q] for q in whole] if r < FINE_ROUNDS else [whole]:
+                if 0 <= r - 1 < V_ROUNDS:
                     load_v(r - 1, part)
                 if r < ROUNDS:
                     load_attn(r, part)

@@ -24,6 +24,9 @@ S_STORE = 2
 ROUNDS = B * S // S_RUN
 T_HI = P // (H * S_RUN)
 T_LO = T // T_HI
+ROW_HI = P // S_RUN
+ROW_LO = T // ROW_HI
+H_BANK = H // S_RUN
 TL_BANK = 8
 PSUM_BANKS = 8
 LOAD_BUFS = 5
@@ -54,11 +57,11 @@ def tile_localtemporalattention_pa_kernel(tc, attn, v, W_out_words, W_out_scales
         def load_attn(r, quarters):
             b, s0 = batch_and_location(r)
             if r not in attn_sb:
-                attn_sb[r] = loads.tile([P, T_LO * T], BF16, name="attn_sb")
-            cols = slice(quarters[0] * TL_BANK * T, (quarters[-1] + 1) * TL_BANK * T)
+                attn_sb[r] = loads.tile([P, H, ROW_LO * T], BF16, name="attn_sb")
+            heads = slice(quarters[0] * H_BANK, (quarters[-1] + 1) * H_BANK)
             nc.sync.dma_start(
-                out=attn_sb[r][:, cols],
-                in_=attn[b, :, s0 : s0 + S_RUN].rearrange("h s (th tl) u -> (s th) h (tl u)", tl=T_LO)[:, :, cols],
+                out=attn_sb[r][:, heads],
+                in_=attn[b, heads, s0 : s0 + S_RUN].rearrange("h s (th tl) u -> (s th) h (tl u)", tl=ROW_LO),
             )
 
         def load_v(r, locations):
@@ -111,9 +114,11 @@ def tile_localtemporalattention_pa_kernel(tc, attn, v, W_out_words, W_out_scales
                         stop=True,
                     )
                 if turns:
-                    tl = sl * TL_BANK + i
+                    tl, head = divmod(i, H_BANK)
                     nc.tensor.transpose(
-                        out=attnT_ps[:, i, :], in_=attn_sb[r + 1][:, tl * T : (tl + 1) * T], identity=by_head[:]
+                        out=attnT_ps[:, i, :],
+                        in_=attn_sb[r + 1][:, sl * H_BANK + head, tl * T : (tl + 1) * T],
+                        identity=ident_bf16[:],
                     )
             if mixes:
                 if sl == 0:
@@ -124,10 +129,10 @@ def tile_localtemporalattention_pa_kernel(tc, attn, v, W_out_words, W_out_scales
                 )
             if turns:
                 if sl == 0:
-                    attnT[r + 1] = work.tile([P, H * S_RUN, T_LO, T_HI], BF16, name="attnT")
+                    attnT[r + 1] = work.tile([P, H * S_RUN, ROW_LO, ROW_HI], BF16, name="attnT")
                 nc.scalar.copy(
-                    out=attnT[r + 1][:].bitcast(F32)[:, :, sl * TL_BANK : (sl + 1) * TL_BANK, :],
-                    in_=attnT_ps[:].bitcast(F32).rearrange("u tl (hs w) -> u hs tl w", w=T_HI // 2),
+                    out=attnT[r + 1][:].bitcast(F32)[:, sl * TL_BANK : (sl + 1) * TL_BANK],
+                    in_=attnT_ps[:].bitcast(F32).rearrange("u (tl h) (s w) -> u (h s) tl w", h=H_BANK, s=S_RUN),
                 )
 
         def transpose_ctx(r, sl):
@@ -136,7 +141,7 @@ def tile_localtemporalattention_pa_kernel(tc, attn, v, W_out_words, W_out_scales
             ctxT_ps = psum.tile([P, G, 2, P], F32, name="ctxT_ps", tag="bank")
             for g in range(G):
                 for w in range(2):
-                    nc.tensor.transpose(out=ctxT_ps[:, g, w, :], in_=ctx_words[r][:, sl, g, w, :], identity=ident[:])
+                    nc.tensor.transpose(out=ctxT_ps[:, g, w, :], in_=ctx_words[r][:, sl, g, w, :], identity=by_row[:])
             nc.scalar.copy(out=grouped[r][:, sl].bitcast(F32), in_=ctxT_ps[:].rearrange("p g w m -> p g m w"))
 
         def quantise(r, first):
@@ -187,9 +192,12 @@ def tile_localtemporalattention_pa_kernel(tc, attn, v, W_out_words, W_out_scales
                 load_weight()
         ident = const.tile([P, P], F32, name="ident")
         make_identity(nc, ident[:])
-        by_head = const.tile([P, P], BF16, name="by_head")
+        ident_bf16 = const.tile([P, P], BF16, name="ident_bf16")
+        nc.vector.tensor_copy(out=ident_bf16[:], in_=ident[:])
+        by_row = const.tile([P, P], F32, name="by_row")
         nc.vector.tensor_copy(
-            out=by_head[:].rearrange("i (h x) -> i h x", h=H), in_=ident[:].rearrange("i (x h) -> i h x", h=H)
+            out=by_row[:].rearrange("i (a lo q) -> i a lo q", lo=ROW_LO, q=T_HI),
+            in_=ident[:].rearrange("i (lo q a) -> i a lo q", lo=ROW_LO, q=T_HI),
         )
 
         half = S_RUN // 2

from contextlib import ExitStack

import concourse.mybir as mybir
from concourse.masks import make_identity

BF16 = mybir.dt.bfloat16
F32 = mybir.dt.float32
I32 = mybir.dt.int32
U32 = mybir.dt.uint32
U8 = mybir.dt.uint8
FP8X4 = mybir.dt.float8_e4m3fn_x4
FP4X4 = mybir.dt.float4_e2m1fn_x4

B, T, S, H, HD = 2, 128, 16, 8, 128
C = H * HD
CO = 1024
P = 128
K_PASS = 4 * P
G = C // K_PASS
N_MX = 512

S_RUN = 4
S_STORE = 2
ROUNDS = B * S // S_RUN
T_HI = P // (H * S_RUN)
T_LO = T // T_HI
ROW_HI = P // S_RUN
ROW_LO = T // ROW_HI
H_BANK = H // S_RUN
TL_BANK = 8
PSUM_BANKS = 8
LOAD_BUFS = 5
V_ROUNDS = 2
FINE_ROUNDS = 4

assert TL_BANK == H and S_RUN * TL_BANK == T_LO

FLOPS = 2 * B * T * S * C * CO + 2 * B * H * S * T * T * HD


def tile_localtemporalattention_pa_kernel(tc, attn, v, W_out_words, W_out_scales, out):
    nc = tc.nc
    with ExitStack() as stack:
        const = stack.enter_context(tc.tile_pool(name="const", bufs=1))
        loads = stack.enter_context(tc.tile_pool(name="loads", bufs=LOAD_BUFS))
        v_loads = stack.enter_context(tc.tile_pool(name="v_loads", bufs=3))
        work = stack.enter_context(tc.tile_pool(name="work", bufs=2))
        stage = stack.enter_context(tc.tile_pool(name="stage", bufs=6))
        psum = stack.enter_context(tc.psum_pool(name="psum", bufs=PSUM_BANKS))
        stack.enter_context(tc.manual_schedule())

        attn_sb, v_sb, v_pairs, attnT, ctx_words, grouped, codes, code_scales, out_sb = {}, {}, {}, {}, {}, {}, {}, {}, {}

        def batch_and_location(r):
            return divmod(r * S_RUN, S)

        def load_attn(r, quarters):
            b, s0 = batch_and_location(r)
            if r not in attn_sb:
                attn_sb[r] = loads.tile([P, H, ROW_LO * T], BF16, name="attn_sb")
            heads = slice(quarters[0] * H_BANK, (quarters[-1] + 1) * H_BANK)
            nc.sync.dma_start(
                out=attn_sb[r][:, heads],
                in_=attn[b, heads, s0 : s0 + S_RUN].rearrange("h s (th tl) u -> (s th) h (tl u)", tl=ROW_LO),
            )

        def load_v(r, locations):
            b, s0 = batch_and_location(r)
            if r % V_ROUNDS == 0 and r not in v_sb:
                tile = v_loads.tile([P, V_ROUNDS * S_RUN, C], BF16, name="v_pair")
                for i in range(V_ROUNDS):
                    v_sb[r + i] = tile[:, i * S_RUN : (i + 1) * S_RUN]
                v_pairs[r // V_ROUNDS] = tile
            first, last = locations[0], locations[-1] + 1
            shift = r % V_ROUNDS * S_RUN
            nc.sync.dma_start(
                out=v_pairs[r // V_ROUNDS][:, shift + first : shift + last],
                in_=v[b, :, s0 + first : s0 + last].rearrange("u s h d -> u s (h d)"),
            )

        def load_pair(r):
            whole = list(range(S_RUN))
            if r - 1 >= V_ROUNDS and (r - 1) % V_ROUNDS == 0 and r - 1 < ROUNDS:
                load_v(r - 1, list(range(V_ROUNDS * S_RUN)))
            for part in [[q] for q in whole] if r < FINE_ROUNDS else [whole]:
                if 0 <= r - 1 < V_ROUNDS:
                    load_v(r - 1, part)
                if r < ROUNDS:
                    load_attn(r, part)

        def load_weight():
            for quadrant in range(4):
                rows = slice(4 * quadrant, 4 * quadrant + 4)
                nc.sync.dma_start(
                    out=w_planes[32 * quadrant : 32 * quadrant + 4].bitcast(I32),
                    in_=W_out_scales[:, rows, :].rearrange("g q n -> q g n").bitcast(I32),
                )
            for g in range(G):
                nc.sync.dma_start(out=w_words[:, g, :].bitcast(I32), in_=W_out_words[g].bitcast(I32))

        def mix_and_transpose(r, sl):
            mixes, turns = 0 <= r < ROUNDS, r + 1 < ROUNDS
            if mixes:
                ctx_ps = psum.tile([P, C], BF16, name="ctx_ps", tag="bank")
            if turns:
                attnT_ps = psum.tile([P, TL_BANK, P], BF16, name="attnT_ps", tag="bank")
            for i in range(H):
                if mixes:
                    nc.tensor.matmul(
                        out=ctx_ps[:, i * HD : (i + 1) * HD],
                        lhsT=attnT[r][:, i * S_RUN + sl].rearrange("u tl th -> u (tl th)"),
                        rhs=v_sb[r][:, sl, i * HD : (i + 1) * HD],
                        start=True,
                        stop=True,
                    )
                if turns:
                    tl, head = divmod(i, H_BANK)
                    nc.tensor.transpose(
                        out=attnT_ps[:, i, :],
                        in_=attn_sb[r + 1][:, sl * H_BANK + head, tl * T : (tl + 1) * T],
                        identity=ident_bf16[:],
                    )
            if mixes:
                if sl == 0:
                    ctx_words[r] = work.tile([P, S_RUN, G, 2, P], F32, name="ctx_words")
                nc.vector.tensor_copy(
                    out=ctx_words[r][:, sl],
                    in_=ctx_ps[:].bitcast(F32).rearrange("m (g p w) -> m g w p", g=G, w=2),
                )
            if turns:
                if sl == 0:
                    attnT[r + 1] = work.tile([P, H * S_RUN, ROW_LO, ROW_HI], BF16, name="attnT")
                nc.scalar.copy(
                    out=attnT[r + 1][:].bitcast(F32)[:, sl * TL_BANK : (sl + 1) * TL_BANK],
                    in_=attnT_ps[:].bitcast(F32).rearrange("u (tl h) (s w) -> u (h s) tl w", h=H_BANK, s=S_RUN),
                )

        def transpose_ctx(r, sl):
            if sl == 0:
                grouped[r] = work.tile([P, S_RUN, G, P, 4], BF16, name="grouped", align_bytes=64)
            ctxT_ps = psum.tile([P, G, 2, P], F32, name="ctxT_ps", tag="bank")
            for g in range(G):
                for w in range(2):
                    nc.tensor.transpose(out=ctxT_ps[:, g, w, :], in_=ctx_words[r][:, sl, g, w, :], identity=by_row[:])
            nc.scalar.copy(out=grouped[r][:, sl].bitcast(F32), in_=ctxT_ps[:].rearrange("p g w m -> p g m w"))

        def quantise(r, first):
            if first == 0:
                codes[r] = work.tile([P, S_RUN * G * P], U32, name="codes", align_bytes=64)
                code_scales[r] = work.tile([P, S_RUN * G * P], U8, name="code_scales", align_bytes=64)
            cols = slice(first * G * P, (first + S_STORE) * G * P)
            nc.vector.quantize_mx(
                out=codes[r][:, cols].bitcast(FP8X4),
                scales=code_scales[r][:, cols],
                in_=grouped[r][:, first : first + S_STORE].rearrange("p s g m j -> p (s g m j)"),
            )

        def project(r, sl, width):
            b, s0 = batch_and_location(r)
            i = sl % width
            if i == 0:
                out_sb[r] = stage.tile([P, width, CO], F32, name="out_sb")
            for n0 in range(0, CO, N_MX):
                acc = psum.tile([P, N_MX], F32, name="acc", tag="bank")
                for g in range(G):
                    rows = slice((sl * G + g) * P, (sl * G + g + 1) * P)
                    nc.tensor.matmul_mx(
                        out=acc[:],
                        lhsT=codes[r][:, rows].bitcast(FP8X4),
                        lhsT_scale=code_scales[r][:, rows],
                        rhs=w_words[:, g, 2 * n0 : 2 * (n0 + N_MX)].bitcast(FP4X4),
                        rhs_scale=w_planes[:, g, n0 : n0 + N_MX],
                        start=(g == 0),
                        stop=(g == G - 1),
                    )
                if n0 == 0:
                    nc.scalar.copy(out=out_sb[r][:, i, n0 : n0 + N_MX], in_=acc[:])
                else:
                    nc.vector.tensor_copy(out=out_sb[r][:, i, n0 : n0 + N_MX], in_=acc[:])
            if i == width - 1:
                s = s0 + sl - i
                rows_of_t = out[b].rearrange("(th tl s) c -> tl th (s c)", th=T_HI, tl=T_LO)
                queue = nc.gpsimd if r < ROUNDS - 1 else nc.sync
                queue.dma_start(out=rows_of_t[:, :, s * CO : (s + width) * CO], in_=out_sb[r][:])

        w_words = const.tile([P, G, 2 * CO], U8, name="w_words", align_bytes=64)
        w_planes = const.tile([P, G, CO], U8, name="w_planes", align_bytes=64)
        nc.vector.memset(w_planes[:].bitcast(I32), 0)
        for r in range(LOAD_BUFS):
            load_pair(r)
            if r == 1:
                load_weight()
        ident = const.tile([P, P], F32, name="ident")
        make_identity(nc, ident[:])
        ident_bf16 = const.tile([P, P], BF16, name="ident_bf16")
        nc.vector.tensor_copy(out=ident_bf16[:], in_=ident[:])
        by_row = const.tile([P, P], F32, name="by_row")
        nc.vector.tensor_copy(
            out=by_row[:].rearrange("i (a lo q) -> i a lo q", lo=ROW_LO, q=T_HI),
            in_=ident[:].rearrange("i (lo q a) -> i a lo q", lo=ROW_LO, q=T_HI),
        )

        half = S_RUN // 2
        for p in range(-1, ROUNDS + 1):
            here, before = 0 <= p < ROUNDS, 0 <= p - 1 < ROUNDS
            for sl in range(S_RUN):
                mix_and_transpose(p, sl)
                if here and sl >= half:
                    transpose_ctx(p, sl - half)
            if p + LOAD_BUFS < ROUNDS:
                load_pair(p + 1 + LOAD_BUFS)
            if here:
                quantise(p, 0)
            if before:
                for sl in range(half, S_RUN):
                    project(p - 1, sl, S_STORE if p - 1 < ROUNDS - 1 else 1)
            if here:
                for sl in range(half, S_RUN):
                    transpose_ctx(p, sl)
                quantise(p, half)
                for sl in range(half):
                    project(p, sl, S_STORE if p < ROUNDS - 1 else 1)
